import numpy as np
import ml_dtypes


def mxq(x, axis, fmt="e4m3"):
    dtype, down = {"e4m3": (ml_dtypes.float8_e4m3fn, 7), "e5m2": (ml_dtypes.float8_e5m2, 14)}[fmt]
    v = np.moveaxis(np.asarray(x, np.float32).astype(ml_dtypes.bfloat16).astype(np.float64), axis, -1)
    blocks = v.reshape(v.shape[:-1] + (-1, 32))
    amax = np.abs(blocks).max(-1, keepdims=True)
    byte = np.maximum(np.where(amax > 0, np.frexp(amax)[1] - 1 + 127, 0) - down, 1)
    scale = np.exp2(byte - 127.0)
    codes = (blocks / scale).astype(np.float32).astype(dtype).astype(np.float64)
    return np.moveaxis((codes * scale).reshape(v.shape), -1, axis)


WIDE = False


def mx_kscale(k):
    if not WIDE:
        return np.ones(k)
    levels = np.array([10, -10, 5, -5, 0])
    a = np.random.permutation(np.resize(levels, k // 512 * 4)).reshape(k // 512, 4)
    idx = np.arange(k)
    return np.exp2(a[idx // 512, idx % 128 // 32])


BF16 = ml_dtypes.bfloat16


def bf(x):
    return np.asarray(x, np.float32).astype(BF16)


def f64(x):
    return np.asarray(x).astype(np.float64)


B, T, C, H, KH, D = 4, 1024, 1024, 4, 4, 128
HD = H * D


def sigmoid(v):
    return 1.0 / (1.0 + np.exp(-v))


def setup_inputs():
    s, t = mx_kscale(C), mx_kscale(HD)
    return {"x": bf(np.random.standard_normal((B, T, C)) * s),
            "y_attn": bf((np.random.standard_normal((B, T, HD)) * 0.3 * t).reshape(B, T, H, D)),
            "w_gate": bf(np.random.standard_normal((C, HD)) / np.sqrt(C) / s[:, None]),
            "w_proj": bf(np.random.standard_normal((HD, C)) * 3.0 / np.sqrt(HD) / t[:, None])}


def reference(x, y_attn, w_gate, w_proj):
    gate = sigmoid((mxq(f64(x), 2, "e4m3") @ mxq(f64(w_gate), 0, "e4m3")).reshape(B, T, H, D))
    y = f64(y_attn) * gate
    return mxq(y.reshape(B, T, HD), 2, "e4m3") @ mxq(f64(w_proj), 0, "e4m3")

@@ -1,0 +1,291 @@
+from contextlib import ExitStack
+
+import concourse.mybir as mybir
+from concourse.masks import make_identity
+
+FLOPS = 2 * 4096 * 1024 * 512 * 2
+
+BF16 = mybir.dt.bfloat16
+F32 = mybir.dt.float32
+U32 = mybir.dt.uint32
+U8 = mybir.dt.uint8
+FP8X4 = mybir.dt.float8_e4m3fn_x4
+SIGMOID = mybir.ActivationFunctionType.Sigmoid
+MULT = mybir.AluOpType.mult
+
+P = 128
+NG = 8
+NU = 16
+K1 = 2
+K2 = 12
+VSET = [3]
+PRELOAD = 4
+SPLIT_LAST = 1
+
+
+def tile_multiheadattention_pb_t_kernel(tc, x, y_attn, w_gate, w_proj, out):
+    nc = tc.nc
+    xv = x.rearrange("b (s p i) c -> (b s) p (i c)", p=P, i=4)
+    yv = y_attn.rearrange("b (s p i) h d -> (b s) p (i h d)", p=P, i=4)
+    ov = out.rearrange("b (s p i) n -> (b s) p (i n)", p=P, i=4)
+
+    with ExitStack() as ctx:
+        const = ctx.enter_context(tc.tile_pool(name="const", bufs=1))
+        xpool = ctx.enter_context(tc.tile_pool(name="xpool", bufs=6))
+        ypool = ctx.enter_context(tc.tile_pool(name="ypool", bufs=6))
+        opool = ctx.enter_context(tc.tile_pool(name="opool", bufs=8))
+        work = ctx.enter_context(tc.tile_pool(name="work", bufs=3))
+        ps_x = ctx.enter_context(tc.psum_pool(name="ps_x", bufs=2))
+        ps_y = ctx.enter_context(tc.psum_pool(name="ps_y", bufs=1))
+        ps_g = ctx.enter_context(tc.psum_pool(name="ps_g", bufs=2))
+        ps_o = ctx.enter_context(tc.psum_pool(name="ps_o", bufs=3))
+        ctx.enter_context(tc.manual_schedule())
+
+        x_sb = {}
+        y_sb = {}
+        xt = {}
+        yt = {}
+        gt = {}
+        ot = {}
+        xgrp = {}
+        xc = {}
+        xs = {}
+        sig = {}
+        hgrp = {}
+        hc = {}
+        hs = {}
+        ost = {}
+
+        def copy_on(eng, dst, src):
+            if eng == "V":
+                nc.vector.tensor_copy(out=dst, in_=src)
+            else:
+                nc.scalar.copy(out=dst, in_=src)
+
+        def load(g):
+            if g >= NG:
+                return
+            x_sb[g] = xpool.tile([P, 4096], BF16, name="x_sb")
+            nc.sync.dma_start(out=x_sb[g][:], in_=xv[g])
+            y_sb[g] = ypool.tile([P, 2048], BF16, name="y_sb")
+            nc.sync.dma_start(out=y_sb[g][:], in_=yv[g])
+
+        warm = const.tile([P, 1], F32, name="warm")
+        warm2 = const.tile([P, 1], F32, name="warm2")
+        nc.vector.memset(warm[:], 0.0)
+        nc.scalar.activation(out=warm2[:], in_=warm[:], func=SIGMOID)
+        ident = const.tile([P, P], F32, name="ident")
+        make_identity(nc, ident[:])
+
+        wgc = const.tile([P, 1024], U32, name="wgc", align_bytes=64)
+        wgs = const.tile([P, 1024], U8, name="wgs", align_bytes=64)
+        wpc = const.tile([P, 1024], U32, name="wpc", align_bytes=64)
+        wps = const.tile([P, 1024], U8, name="wps", align_bytes=64)
+
+        wg_raw = opool.tile([P, 4096], BF16, name="wg_raw", tag="ost", align_bytes=64)
+        wgv = w_gate.rearrange("(a q e) m -> q a (e m)", a=4, q=P, e=2)
+        for g2 in range(2):
+            nc.sync.dma_start(
+                out=wg_raw[:, 2048 * g2 : 2048 * g2 + 2048].rearrange("p (a r) -> p a r", a=2),
+                in_=wgv[:, 2 * g2 : 2 * g2 + 2, :],
+            )
+        load(0)
+        wp_raw = opool.tile([P, 4096], BF16, name="wp_raw", tag="ost", align_bytes=64)
+        nc.sync.dma_start(
+            out=wp_raw[:].rearrange("p (u r) -> p u r", u=2),
+            in_=w_proj.rearrange("(u q e) n -> q u (e n)", u=2, q=P, e=2),
+        )
+        for g in range(1, PRELOAD):
+            load(g)
+
+        wg_grp = opool.tile([P, 4096], BF16, name="wg_grp", tag="ost", align_bytes=64)
+
+        def wg_regroup(eng, g2, u2):
+            src = wg_raw[:, 2048 * g2 : 2048 * g2 + 2048].rearrange("p (j m) -> p j m", j=4)
+            base = 2048 * g2 + 1024 * u2
+            copy_on(
+                eng,
+                wg_grp[:, base : base + 1024].rearrange("p (e2 p2 j) -> p e2 p2 j", e2=2, j=4),
+                src[:, :, 256 * u2 : 256 * u2 + 256].rearrange("p j (p2 e2) -> p e2 p2 j", e2=2),
+            )
+
+        wg_regroup("V", 0, 0)
+        wg_regroup("V", 0, 1)
+        wg_regroup("S", 1, 1)
+        wg_regroup("V", 1, 0)
+        for g2 in range(2):
+            nc.vector.quantize_mx(
+                out=wgc[:, 512 * g2 : 512 * g2 + 512].bitcast(FP8X4),
+                scales=wgs[:, 512 * g2 : 512 * g2 + 512],
+                in_=wg_grp[:, 2048 * g2 : 2048 * g2 + 2048],
+            )
+
+        wp_grp = opool.tile([P, 4096], BF16, name="wp_grp", tag="ost", align_bytes=64)
+
+        def wp_prepare():
+            for q in range(2):
+                nc.vector.tensor_copy(
+                    out=wp_grp[:, 2048 * q : 2048 * q + 2048].rearrange(
+                        "p (c i t) -> p c t i", i=4, t=4
+                    ),
+                    in_=wp_raw[:]
+                    .rearrange("p (t n) -> p t n", t=4)[:, :, 512 * q : 512 * q + 512]
+                    .rearrange("p t (c i) -> p c t i", i=4),
+                )
+            nc.vector.quantize_mx(out=wpc[:].bitcast(FP8X4), scales=wps[:], in_=wp_grp[:])
+
+        def live(k):
+            return 0 <= k < NU
+
+        def t_x(k):
+            if not live(k):
+                return
+            x32 = x_sb[k // 2][:].bitcast(F32)
+            for b in range(2):
+                i = 2 * (k % 2) + b
+                xt[(k, b)] = ps_x.tile([P, 512], F32, name="xt")
+                for a in range(4):
+                    nc.tensor.transpose(
+                        xt[(k, b)][:, 128 * a : 128 * a + 128],
+                        x32[:, 512 * i + 128 * a : 512 * i + 128 * a + 128],
+                        ident[:],
+                    )
+
+        def c_x(k):
+            if not live(k):
+                return
+            xgrp[k] = work.tile([P, 2048], BF16, name="xgrp", align_bytes=64)
+            xg32 = xgrp[k][:].bitcast(F32).rearrange("p (g t u) -> p g t u", g=2, u=2)
+            for b in range(2):
+                copy_on(
+                    "S" if k < K1 else "V",
+                    xg32[:, :, 128 * b : 128 * b + 128, :],
+                    xt[(k, b)][:].rearrange("p (g u t) -> p g t u", g=2, u=2),
+                )
+
+        def q_x(k):
+            if not live(k):
+                return
+            xc[k] = work.tile([P, 512], U32, name="xc", align_bytes=64)
+            xs[k] = work.tile([P, 512], U8, name="xs", align_bytes=64)
+            nc.vector.quantize_mx(out=xc[k][:].bitcast(FP8X4), scales=xs[k][:], in_=xgrp[k][:])
+
+        def mm1(k):
+            if not live(k):
+                return
+            for u2 in range(2):
+                gt[(k, u2)] = ps_g.tile([P, 512], F32, name="gt")
+                for e2 in range(2):
+                    m = 2 * u2 + e2
+                    for g2 in range(2):
+                        wcols = slice(512 * g2 + 128 * m, 512 * g2 + 128 * m + 128)
+                        xcols = slice(256 * g2, 256 * g2 + 256)
+                        nc.tensor.matmul_mx(
+                            out=gt[(k, u2)][:, 256 * e2 : 256 * e2 + 256],
+                            lhsT=wgc[:, wcols].bitcast(FP8X4),
+                            lhsT_scale=wgs[:, wcols],
+                            rhs=xc[k][:, xcols].bitcast(FP8X4),
+                            rhs_scale=xs[k][:, xcols],
+                            start=(g2 == 0),
+                            stop=(g2 == 1),
+                        )
+
+        def s_g(k):
+            if not live(k):
+                return
+            sig[k] = work.tile([P, 1024], F32, name="sig")
+            for u2 in range(2):
+                nc.scalar.activation(
+                    out=sig[k][:, 512 * u2 : 512 * u2 + 512], in_=gt[(k, u2)][:], func=SIGMOID
+                )
+
+        def t_y(k):
+            if not live(k):
+                return
+            y32 = y_sb[k // 2][:].bitcast(F32)
+            yt[k] = ps_y.tile([P, 512], F32, name="yt")
+            for b in range(2):
+                i = 2 * (k % 2) + b
+                for u in range(2):
+                    nc.tensor.transpose(
+                        yt[k][:, 256 * u + 128 * b : 256 * u + 128 * b + 128],
+                        y32[:, 256 * i + 128 * u : 256 * i + 128 * u + 128],
+                        ident[:],
+                    )
+
+        def mul(k):
+            if not live(k):
+                return
+            hgrp[k] = work.tile([P, 1024], BF16, name="hgrp", align_bytes=64)
+            nc.vector.tensor_tensor(
+                out=hgrp[k][:].rearrange("p (t u e) -> p t u e", u=2, e=2),
+                in0=sig[k][:].rearrange("p (u e t) -> p t u e", u=2, e=2),
+                in1=yt[k][:].bitcast(BF16).rearrange("p (u t e) -> p t u e", u=2, e=2),
+                op=MULT,
+            )
+
+        def q_h(k):
+            if not live(k):
+                return
+            hc[k] = work.tile([P, 256], U32, name="hc", align_bytes=64)
+            hs[k] = work.tile([P, 256], U8, name="hs", align_bytes=64)
+            nc.vector.quantize_mx(out=hc[k][:].bitcast(FP8X4), scales=hs[k][:], in_=hgrp[k][:])
+
+        def mm2(k, js):
+            if not live(k):
+                return
+            for j in js:
+                b = j // 2
+                n2 = j % 2
+                tcols = slice(128 * b, 128 * b + 128)
+                ncols = slice(512 * n2, 512 * n2 + 512)
+                ot[(k, j)] = ps_o.tile([P, 512], F32, name="ot")
+                nc.tensor.matmul_mx(
+                    out=ot[(k, j)][:],
+                    lhsT=hc[k][:, tcols].bitcast(FP8X4),
+                    lhsT_scale=hs[k][:, tcols],
+                    rhs=wpc[:, ncols].bitcast(FP8X4),
+                    rhs_scale=wps[:, ncols],
+                    start=True,
+                    stop=True,
+                )
+
+        def c_o(k, js):
+            if not live(k):
+                return
+            if js[0] == 0:
+                ost[k] = opool.tile([P, 2048], F32, name="ost", tag="ost", align_bytes=64)
+            for j in js:
+                copy_on(
+                    "V" if (k >= K2 and j in VSET) else "S",
+                    ost[k][:, 512 * j : 512 * j + 512],
+                    ot[(k, j)][:],
+                )
+
+        def store(k):
+            if not live(k):
+                return
+            dst = ov[k // 2][:, 2048 * (k % 2) : 2048 * (k % 2) + 2048]
+            parts = 4 if k >= NU - SPLIT_LAST else 1
+            w = 2048 // parts
+            for q in range(parts):
+                nc.sync.dma_start(out=dst[:, w * q : w * q + w], in_=ost[k][:, w * q : w * q + w])
+
+        for t in range(NU + 5):
+            t_y(t - 2)
+            t_x(t)
+            if t == 2:
+                wp_prepare()
+            c_x(t)
+            c_o(t - 4, [2, 3])
+            store(t - 4)
+            if t >= 4 and t % 2 == 0:
+                load(t // 2 + PRELOAD - 2)
+            s_g(t - 2)
+            mul(t - 2)
+            mm2(t - 3, [0, 1])
+            c_o(t - 3, [0, 1])
+            q_x(t)
+            mm1(t - 1)
+            q_h(t - 2)
+            mm2(t - 3, [2, 3])

@@ -16,11 +16,7 @@ MULT = mybir.AluOpType.mult
 P = 128
 NG = 8
 NU = 16
-K1 = 2
-K2 = 12
-VSET = [3]
-PRELOAD = 4
-SPLIT_LAST = 1
+PRELOAD = 8
 
 
 def tile_multiheadattention_pb_t_kernel(tc, x, y_attn, w_gate, w_proj, out):
@@ -31,8 +27,8 @@ def tile_multiheadattention_pb_t_kernel(tc, x, y_attn, w_gate, w_proj, out):
 
     with ExitStack() as ctx:
         const = ctx.enter_context(tc.tile_pool(name="const", bufs=1))
-        xpool = ctx.enter_context(tc.tile_pool(name="xpool", bufs=6))
-        ypool = ctx.enter_context(tc.tile_pool(name="ypool", bufs=6))
+        xpool = ctx.enter_context(tc.tile_pool(name="xpool", bufs=8))
+        ypool = ctx.enter_context(tc.tile_pool(name="ypool", bufs=8))
         opool = ctx.enter_context(tc.tile_pool(name="opool", bufs=8))
         work = ctx.enter_context(tc.tile_pool(name="work", bufs=3))
         ps_x = ctx.enter_context(tc.psum_pool(name="ps_x", bufs=2))
@@ -137,31 +133,36 @@ def tile_multiheadattention_pb_t_kernel(tc, x, y_attn, w_gate, w_proj, out):
         def live(k):
             return 0 <= k < NU
 
-        def t_x(k):
+        def cx_engine(k, b):
+            return "S"
+
+        def co_engine(k, j):
+            return "V" if (j == 3 or (j == 2 and k % 2 == 1)) else "S"
+
+        def t_x(k, b):
             if not live(k):
                 return
             x32 = x_sb[k // 2][:].bitcast(F32)
-            for b in range(2):
-                i = 2 * (k % 2) + b
-                xt[(k, b)] = ps_x.tile([P, 512], F32, name="xt")
-                for a in range(4):
-                    nc.tensor.transpose(
-                        xt[(k, b)][:, 128 * a : 128 * a + 128],
-                        x32[:, 512 * i + 128 * a : 512 * i + 128 * a + 128],
-                        ident[:],
-                    )
+            i = 2 * (k % 2) + b
+            xt[(k, b)] = ps_x.tile([P, 512], F32, name="xt")
+            for a in range(4):
+                nc.tensor.transpose(
+                    xt[(k, b)][:, 128 * a : 128 * a + 128],
+                    x32[:, 512 * i + 128 * a : 512 * i + 128 * a + 128],
+                    ident[:],
+                )
 
-        def c_x(k):
+        def c_x(k, b):
             if not live(k):
                 return
-            xgrp[k] = work.tile([P, 2048], BF16, name="xgrp", align_bytes=64)
+            if b == 0:
+                xgrp[k] = work.tile([P, 2048], BF16, name="xgrp", align_bytes=64)
             xg32 = xgrp[k][:].bitcast(F32).rearrange("p (g t u) -> p g t u", g=2, u=2)
-            for b in range(2):
-                copy_on(
-                    "S" if k < K1 else "V",
-                    xg32[:, :, 128 * b : 128 * b + 128, :],
-                    xt[(k, b)][:].rearrange("p (g u t) -> p g t u", g=2, u=2),
-                )
+            copy_on(
+                cx_engine(k, b),
+                xg32[:, :, 128 * b : 128 * b + 128, :],
+                xt[(k, b)][:].rearrange("p (g u t) -> p g t u", g=2, u=2),
+            )
 
         def q_x(k):
             if not live(k):
@@ -256,36 +257,45 @@ def tile_multiheadattention_pb_t_kernel(tc, x, y_attn, w_gate, w_proj, out):
             if js[0] == 0:
                 ost[k] = opool.tile([P, 2048], F32, name="ost", tag="ost", align_bytes=64)
             for j in js:
-                copy_on(
-                    "V" if (k >= K2 and j in VSET) else "S",
-                    ost[k][:, 512 * j : 512 * j + 512],
-                    ot[(k, j)][:],
-                )
+                copy_on(co_engine(k, j), ost[k][:, 512 * j : 512 * j + 512], ot[(k, j)][:])
 
-        def store(k):
+        def store(k, cols):
             if not live(k):
                 return
             dst = ov[k // 2][:, 2048 * (k % 2) : 2048 * (k % 2) + 2048]
-            parts = 4 if k >= NU - SPLIT_LAST else 1
-            w = 2048 // parts
-            for q in range(parts):
-                nc.sync.dma_start(out=dst[:, w * q : w * q + w], in_=ost[k][:, w * q : w * q + w])
+            nc.sync.dma_start(out=dst[:, cols], in_=ost[k][:, cols])
 
-        for t in range(NU + 5):
-            t_y(t - 2)
-            t_x(t)
-            if t == 2:
+        def x_blocks(first, last):
+            blocks = [q for q in range(first, last + 1) if q < 2 * NU]
+            for q in blocks:
+                t_x(q // 2, q % 2)
+            for q in blocks:
+                c_x(q // 2, q % 2)
+
+        x_blocks(0, 3)
+        q_x(0)
+        q_x(1)
+        for t in range(NU + 2):
+            k = t - 2
+            if t == 0:
                 wp_prepare()
-            c_x(t)
-            c_o(t - 4, [2, 3])
-            store(t - 4)
-            if t >= 4 and t % 2 == 0:
-                load(t // 2 + PRELOAD - 2)
-            s_g(t - 2)
-            mul(t - 2)
-            mm2(t - 3, [0, 1])
-            c_o(t - 3, [0, 1])
-            q_x(t)
-            mm1(t - 1)
-            q_h(t - 2)
-            mm2(t - 3, [2, 3])
+            mul(t - 1)
+            mm2(k, [0, 1, 2])
+            c_o(k, [0, 1, 2])
+            if t >= 1:
+                q_x(t + 1)
+            q_h(t - 1)
+            mm1(t)
+            s_g(t)
+            mm2(k, [3])
+            c_o(k, [3])
+            if k == NU - 1:
+                store(k, slice(0, 1024))
+                store(k, slice(1024, 2048))
+            else:
+                store(k, slice(0, 2048))
+            t_y(t)
+            if t == 0:
+                x_blocks(4, 6)
+            else:
+                x_blocks(2 * t + 5, 2 * t + 6)

@@ -85,7 +85,13 @@ def tile_multiheadattention_pb_t_kernel(tc, x, y_attn, w_gate, w_proj, out):
                 out=wg_raw[:, 2048 * g2 : 2048 * g2 + 2048].rearrange("p (a r) -> p a r", a=2),
                 in_=wgv[:, 2 * g2 : 2 * g2 + 2, :],
             )
-        load(0)
+        x_sb[0] = xpool.tile([P, 4096], BF16, name="x_sb")
+        for h in range(2):
+            nc.sync.dma_start(
+                out=x_sb[0][:, 2048 * h : 2048 * h + 2048], in_=xv[0][:, 2048 * h : 2048 * h + 2048]
+            )
+        y_sb[0] = ypool.tile([P, 2048], BF16, name="y_sb")
+        nc.sync.dma_start(out=y_sb[0][:], in_=yv[0])
         wp_raw = opool.tile([P, 4096], BF16, name="wp_raw", tag="ost", align_bytes=64)
         nc.sync.dma_start(
             out=wp_raw[:].rearrange("p (u r) -> p u r", u=2),
@@ -197,7 +203,9 @@ def tile_multiheadattention_pb_t_kernel(tc, x, y_attn, w_gate, w_proj, out):
             sig[k] = work.tile([P, 1024], F32, name="sig")
             for u2 in range(2):
                 nc.scalar.activation(
-                    out=sig[k][:, 512 * u2 : 512 * u2 + 512], in_=gt[(k, u2)][:], func=SIGMOID
+                    out=sig[k][:, 512 * u2 : 512 * u2 + 512].rearrange("p (t e) -> p t e", e=2),
+                    in_=gt[(k, u2)][:].rearrange("p (e t) -> p t e", e=2),
+                    func=SIGMOID,
                 )
 
         def t_y(k):
@@ -220,7 +228,7 @@ def tile_multiheadattention_pb_t_kernel(tc, x, y_attn, w_gate, w_proj, out):
             hgrp[k] = work.tile([P, 1024], BF16, name="hgrp", align_bytes=64)
             nc.vector.tensor_tensor(
                 out=hgrp[k][:].rearrange("p (t u e) -> p t u e", u=2, e=2),
-                in0=sig[k][:].rearrange("p (u e t) -> p t u e", u=2, e=2),
+                in0=sig[k][:].rearrange("p (u t e) -> p t u e", u=2, e=2),
                 in1=yt[k][:].bitcast(BF16).rearrange("p (u t e) -> p t u e", u=2, e=2),
                 op=MULT,
             )
@@ -277,16 +285,21 @@ def tile_multiheadattention_pb_t_kernel(tc, x, y_attn, w_gate, w_proj, out):
         q_x(1)
         for t in range(NU + 2):
             k = t - 2
-            if t == 0:
-                wp_prepare()
             mul(t - 1)
             mm2(k, [0, 1, 2])
             c_o(k, [0, 1, 2])
             if t >= 1:
                 q_x(t + 1)
             q_h(t - 1)
-            mm1(t)
-            s_g(t)
+            if t == 0:
+                mm1(0)
+                s_g(0)
+                mm1(1)
+                s_g(1)
+                wp_prepare()
+            elif t > 1:
+                mm1(t)
+                s_g(t)
             mm2(k, [3])
             c_o(k, [3])
             if k == NU - 1:

@@ -143,7 +143,7 @@ def tile_multiheadattention_pb_t_kernel(tc, x, y_attn, w_gate, w_proj, out):
             return "S"
 
         def co_engine(k, j):
-            return "V" if (j == 3 or (j == 2 and k % 2 == 1)) else "S"
+            return "V" if (j == 3 or (j == 2 and (1 <= k <= 11 or k == 15))) else "S"
 
         def t_x(k, b):
             if not live(k):

@@ -16,7 +16,6 @@ MULT = mybir.AluOpType.mult
 P = 128
 NG = 8
 NU = 16
-PRELOAD = 8
 
 
 def tile_multiheadattention_pb_t_kernel(tc, x, y_attn, w_gate, w_proj, out):
@@ -30,7 +29,7 @@ def tile_multiheadattention_pb_t_kernel(tc, x, y_attn, w_gate, w_proj, out):
         xpool = ctx.enter_context(tc.tile_pool(name="xpool", bufs=8))
         ypool = ctx.enter_context(tc.tile_pool(name="ypool", bufs=8))
         opool = ctx.enter_context(tc.tile_pool(name="opool", bufs=8))
-        work = ctx.enter_context(tc.tile_pool(name="work", bufs=3))
+        work = ctx.enter_context(tc.tile_pool(name="work", bufs=4))
         ps_x = ctx.enter_context(tc.psum_pool(name="ps_x", bufs=2))
         ps_y = ctx.enter_context(tc.psum_pool(name="ps_y", bufs=1))
         ps_g = ctx.enter_context(tc.psum_pool(name="ps_g", bufs=2))
@@ -52,19 +51,18 @@ def tile_multiheadattention_pb_t_kernel(tc, x, y_attn, w_gate, w_proj, out):
         hs = {}
         ost = {}
 
+        def bank(pool, name):
+            return pool.tile([P, 512], F32, name="bank", tag=name)
+
         def copy_on(eng, dst, src):
-            if eng == "V":
+            if eng == "G":
+                nc.gpsimd.tensor_scalar(
+                    out=dst, in0=src, scalar1=1.0, scalar2=0.0, op0=MULT, op1=mybir.AluOpType.add
+                )
+            elif eng == "V":
                 nc.vector.tensor_copy(out=dst, in_=src)
             else:
                 nc.scalar.copy(out=dst, in_=src)
-
-        def load(g):
-            if g >= NG:
-                return
-            x_sb[g] = xpool.tile([P, 4096], BF16, name="x_sb")
-            nc.sync.dma_start(out=x_sb[g][:], in_=xv[g])
-            y_sb[g] = ypool.tile([P, 2048], BF16, name="y_sb")
-            nc.sync.dma_start(out=y_sb[g][:], in_=yv[g])
 
         warm = const.tile([P, 1], F32, name="warm")
         warm2 = const.tile([P, 1], F32, name="warm2")
@@ -79,28 +77,54 @@ def tile_multiheadattention_pb_t_kernel(tc, x, y_attn, w_gate, w_proj, out):
         wps = const.tile([P, 1024], U8, name="wps", align_bytes=64)
 
         wg_raw = opool.tile([P, 4096], BF16, name="wg_raw", tag="ost", align_bytes=64)
+        wp_raw = opool.tile([P, 4096], BF16, name="wp_raw", tag="ost", align_bytes=64)
+        wg_grp = opool.tile([P, 4096], BF16, name="wg_grp", tag="ost", align_bytes=64)
+        wp_grp = opool.tile([P, 4096], BF16, name="wp_grp", tag="ost", align_bytes=64)
         wgv = w_gate.rearrange("(a q e) m -> q a (e m)", a=4, q=P, e=2)
-        for g2 in range(2):
+
+        def load_wg(g2):
             nc.sync.dma_start(
                 out=wg_raw[:, 2048 * g2 : 2048 * g2 + 2048].rearrange("p (a r) -> p a r", a=2),
                 in_=wgv[:, 2 * g2 : 2 * g2 + 2, :],
             )
-        x_sb[0] = xpool.tile([P, 4096], BF16, name="x_sb")
-        for h in range(2):
-            nc.sync.dma_start(
-                out=x_sb[0][:, 2048 * h : 2048 * h + 2048], in_=xv[0][:, 2048 * h : 2048 * h + 2048]
-            )
-        y_sb[0] = ypool.tile([P, 2048], BF16, name="y_sb")
-        nc.sync.dma_start(out=y_sb[0][:], in_=yv[0])
-        wp_raw = opool.tile([P, 4096], BF16, name="wp_raw", tag="ost", align_bytes=64)
-        nc.sync.dma_start(
-            out=wp_raw[:].rearrange("p (u r) -> p u r", u=2),
-            in_=w_proj.rearrange("(u q e) n -> q u (e n)", u=2, q=P, e=2),
-        )
-        for g in range(1, PRELOAD):
-            load(g)
 
-        wg_grp = opool.tile([P, 4096], BF16, name="wg_grp", tag="ost", align_bytes=64)
+        def load_wp():
+            nc.sync.dma_start(
+                out=wp_raw[:].rearrange("p (u r) -> p u r", u=2),
+                in_=w_proj.rearrange("(u q e) n -> q u (e n)", u=2, q=P, e=2),
+            )
+
+        def load_x(g, first, last):
+            if g not in x_sb:
+                x_sb[g] = xpool.tile([P, 4096], BF16, name="x_sb")
+            cols = slice(1024 * first, 1024 * last)
+            nc.sync.dma_start(out=x_sb[g][:, cols], in_=xv[g][:, cols])
+
+        def load_y(g):
+            y_sb[g] = ypool.tile([P, 2048], BF16, name="y_sb")
+            nc.sync.dma_start(out=y_sb[g][:], in_=yv[g])
+
+        load_wg(0)
+        load_x(0, 0, 2)
+        load_wg(1)
+        load_x(0, 2, 4)
+        load_x(1, 0, 2)
+        load_x(1, 2, 4)
+        load_wp()
+        load_y(0)
+        load_x(2, 0, 4)
+        load_y(1)
+        load_x(3, 0, 4)
+        load_y(2)
+        load_x(4, 0, 4)
+        load_y(3)
+        load_x(5, 0, 4)
+        load_y(4)
+        load_x(6, 0, 4)
+        load_y(5)
+        load_x(7, 0, 4)
+        load_y(6)
+        load_y(7)
 
         def wg_regroup(eng, g2, u2):
             src = wg_raw[:, 2048 * g2 : 2048 * g2 + 2048].rearrange("p (j m) -> p j m", j=4)
@@ -111,63 +135,58 @@ def tile_multiheadattention_pb_t_kernel(tc, x, y_attn, w_gate, w_proj, out):
                 src[:, :, 256 * u2 : 256 * u2 + 256].rearrange("p j (p2 e2) -> p e2 p2 j", e2=2),
             )
 
-        wg_regroup("V", 0, 0)
-        wg_regroup("V", 0, 1)
-        wg_regroup("S", 1, 1)
-        wg_regroup("V", 1, 0)
-        for g2 in range(2):
+        def wg_quantise(g2):
             nc.vector.quantize_mx(
                 out=wgc[:, 512 * g2 : 512 * g2 + 512].bitcast(FP8X4),
                 scales=wgs[:, 512 * g2 : 512 * g2 + 512],
                 in_=wg_grp[:, 2048 * g2 : 2048 * g2 + 2048],
             )
 
-        wp_grp = opool.tile([P, 4096], BF16, name="wp_grp", tag="ost", align_bytes=64)
+        def wp_regroup(eng, q):
+            copy_on(
+                eng,
+                wp_grp[:, 2048 * q : 2048 * q + 2048].rearrange("p (c i t) -> p c t i", i=4, t=4),
+                wp_raw[:]
+                .rearrange("p (t n) -> p t n", t=4)[:, :, 512 * q : 512 * q + 512]
+                .rearrange("p t (c i) -> p c t i", i=4),
+            )
 
-        def wp_prepare():
-            for q in range(2):
-                nc.vector.tensor_copy(
-                    out=wp_grp[:, 2048 * q : 2048 * q + 2048].rearrange(
-                        "p (c i t) -> p c t i", i=4, t=4
-                    ),
-                    in_=wp_raw[:]
-                    .rearrange("p (t n) -> p t n", t=4)[:, :, 512 * q : 512 * q + 512]
-                    .rearrange("p t (c i) -> p c t i", i=4),
-                )
-            nc.vector.quantize_mx(out=wpc[:].bitcast(FP8X4), scales=wps[:], in_=wp_grp[:])
+        def wp_quantise(q):
+            nc.vector.quantize_mx(
+                out=wpc[:, 512 * q : 512 * q + 512].bitcast(FP8X4),
+                scales=wps[:, 512 * q : 512 * q + 512],
+                in_=wp_grp[:, 2048 * q : 2048 * q + 2048],
+            )
 
         def live(k):
             return 0 <= k < NU
 
-        def cx_engine(k, b):
-            return "S"
-
-        def co_engine(k, j):
-            return "V" if (j == 3 or (j == 2 and (1 <= k <= 11 or k == 15))) else "S"
-
-        def t_x(k, b):
+        def t_x(q, pool=ps_x, name="xt"):
+            k = q // 2
             if not live(k):
                 return
             x32 = x_sb[k // 2][:].bitcast(F32)
-            i = 2 * (k % 2) + b
-            xt[(k, b)] = ps_x.tile([P, 512], F32, name="xt")
+            i = q % 4
+            xt[q] = bank(pool, name)
             for a in range(4):
                 nc.tensor.transpose(
-                    xt[(k, b)][:, 128 * a : 128 * a + 128],
+                    xt[q][:, 128 * a : 128 * a + 128],
                     x32[:, 512 * i + 128 * a : 512 * i + 128 * a + 128],
                     ident[:],
                 )
 
-        def c_x(k, b):
+        def c_x(q, eng="S"):
+            k = q // 2
             if not live(k):
                 return
-            if b == 0:
+            b = q % 2
+            if k not in xgrp:
                 xgrp[k] = work.tile([P, 2048], BF16, name="xgrp", align_bytes=64)
             xg32 = xgrp[k][:].bitcast(F32).rearrange("p (g t u) -> p g t u", g=2, u=2)
             copy_on(
-                cx_engine(k, b),
+                eng,
                 xg32[:, :, 128 * b : 128 * b + 128, :],
-                xt[(k, b)][:].rearrange("p (g u t) -> p g t u", g=2, u=2),
+                xt[q][:].rearrange("p (g u t) -> p g t u", g=2, u=2),
             )
 
         def q_x(k):
@@ -177,42 +196,41 @@ def tile_multiheadattention_pb_t_kernel(tc, x, y_attn, w_gate, w_proj, out):
             xs[k] = work.tile([P, 512], U8, name="xs", align_bytes=64)
             nc.vector.quantize_mx(out=xc[k][:].bitcast(FP8X4), scales=xs[k][:], in_=xgrp[k][:])
 
-        def mm1(k):
+        def mm1(k, u2):
             if not live(k):
                 return
-            for u2 in range(2):
-                gt[(k, u2)] = ps_g.tile([P, 512], F32, name="gt")
-                for e2 in range(2):
-                    m = 2 * u2 + e2
-                    for g2 in range(2):
-                        wcols = slice(512 * g2 + 128 * m, 512 * g2 + 128 * m + 128)
-                        xcols = slice(256 * g2, 256 * g2 + 256)
-                        nc.tensor.matmul_mx(
-                            out=gt[(k, u2)][:, 256 * e2 : 256 * e2 + 256],
-                            lhsT=wgc[:, wcols].bitcast(FP8X4),
-                            lhsT_scale=wgs[:, wcols],
-                            rhs=xc[k][:, xcols].bitcast(FP8X4),
-                            rhs_scale=xs[k][:, xcols],
-                            start=(g2 == 0),
-                            stop=(g2 == 1),
-                        )
+            gt[(k, u2)] = bank(ps_g, "gt")
+            for e2 in range(2):
+                m = 2 * u2 + e2
+                for g2 in range(2):
+                    wcols = slice(512 * g2 + 128 * m, 512 * g2 + 128 * m + 128)
+                    xcols = slice(256 * g2, 256 * g2 + 256)
+                    nc.tensor.matmul_mx(
+                        out=gt[(k, u2)][:, 256 * e2 : 256 * e2 + 256],
+                        lhsT=wgc[:, wcols].bitcast(FP8X4),
+                        lhsT_scale=wgs[:, wcols],
+                        rhs=xc[k][:, xcols].bitcast(FP8X4),
+                        rhs_scale=xs[k][:, xcols],
+                        start=(g2 == 0),
+                        stop=(g2 == 1),
+                    )
 
-        def s_g(k):
+        def s_g(k, u2):
             if not live(k):
                 return
-            sig[k] = work.tile([P, 1024], F32, name="sig")
-            for u2 in range(2):
-                nc.scalar.activation(
-                    out=sig[k][:, 512 * u2 : 512 * u2 + 512].rearrange("p (t e) -> p t e", e=2),
-                    in_=gt[(k, u2)][:].rearrange("p (e t) -> p t e", e=2),
-                    func=SIGMOID,
-                )
+            if u2 == 0:
+                sig[k] = work.tile([P, 1024], F32, name="sig")
+            nc.scalar.activation(
+                out=sig[k][:, 512 * u2 : 512 * u2 + 512].rearrange("p (t e) -> p t e", e=2),
+                in_=gt[(k, u2)][:].rearrange("p (e t) -> p t e", e=2),
+                func=SIGMOID,
+            )
 
         def t_y(k):
             if not live(k):
                 return
             y32 = y_sb[k // 2][:].bitcast(F32)
-            yt[k] = ps_y.tile([P, 512], F32, name="yt")
+            yt[k] = bank(ps_y, "yt")
             for b in range(2):
                 i = 2 * (k % 2) + b
                 for u in range(2):
@@ -240,75 +258,83 @@ def tile_multiheadattention_pb_t_kernel(tc, x, y_attn, w_gate, w_proj, out):
             hs[k] = work.tile([P, 256], U8, name="hs", align_bytes=64)
             nc.vector.quantize_mx(out=hc[k][:].bitcast(FP8X4), scales=hs[k][:], in_=hgrp[k][:])
 
-        def mm2(k, js):
+        def mm2(k, j):
             if not live(k):
                 return
-            for j in js:
-                b = j // 2
-                n2 = j % 2
-                tcols = slice(128 * b, 128 * b + 128)
-                ncols = slice(512 * n2, 512 * n2 + 512)
-                ot[(k, j)] = ps_o.tile([P, 512], F32, name="ot")
-                nc.tensor.matmul_mx(
-                    out=ot[(k, j)][:],
-                    lhsT=hc[k][:, tcols].bitcast(FP8X4),
-                    lhsT_scale=hs[k][:, tcols],
-                    rhs=wpc[:, ncols].bitcast(FP8X4),
-                    rhs_scale=wps[:, ncols],
-                    start=True,
-                    stop=True,
-                )
+            tcols = slice(128 * (j // 2), 128 * (j // 2) + 128)
+            ncols = slice(512 * (j % 2), 512 * (j % 2) + 512)
+            ot[(k, j)] = bank(ps_o, "ot")
+            nc.tensor.matmul_mx(
+                out=ot[(k, j)][:],
+                lhsT=hc[k][:, tcols].bitcast(FP8X4),
+                lhsT_scale=hs[k][:, tcols],
+                rhs=wpc[:, ncols].bitcast(FP8X4),
+                rhs_scale=wps[:, ncols],
+                start=True,
+                stop=True,
+            )
 
-        def c_o(k, js):
+        def c_o(k, j, eng):
             if not live(k):
                 return
-            if js[0] == 0:
+            if k not in ost:
                 ost[k] = opool.tile([P, 2048], F32, name="ost", tag="ost", align_bytes=64)
-            for j in js:
-                copy_on(co_engine(k, j), ost[k][:, 512 * j : 512 * j + 512], ot[(k, j)][:])
+            copy_on(eng, ost[k][:, 512 * j : 512 * j + 512], ot[(k, j)][:])
 
-        def store(k, cols):
+        def store(k, parts=1):
             if not live(k):
                 return
-            dst = ov[k // 2][:, 2048 * (k % 2) : 2048 * (k % 2) + 2048]
-            nc.sync.dma_start(out=dst[:, cols], in_=ost[k][:, cols])
+            w = 2048 // parts
+            for part in range(parts):
+                lo = w * part
+                base = 2048 * (k % 2) + lo
+                nc.sync.dma_start(out=ov[k // 2][:, base : base + w], in_=ost[k][:, lo : lo + w])
 
-        def x_blocks(first, last):
-            blocks = [q for q in range(first, last + 1) if q < 2 * NU]
-            for q in blocks:
-                t_x(q // 2, q % 2)
-            for q in blocks:
-                c_x(q // 2, q % 2)
-
-        x_blocks(0, 3)
+        wg_regroup("V", 0, 0)
+        wg_regroup("S", 0, 1)
+        for q in range(2):
+            t_x(q)
+        c_x(0, "S")
+        c_x(1, "V")
+        wg_quantise(0)
+        wg_regroup("V", 1, 0)
+        wg_regroup("S", 1, 1)
         q_x(0)
+        wg_quantise(1)
+        for q in range(2, 4):
+            t_x(q)
+        for q in range(2, 4):
+            c_x(q)
         q_x(1)
-        for t in range(NU + 2):
-            k = t - 2
-            mul(t - 1)
-            mm2(k, [0, 1, 2])
-            c_o(k, [0, 1, 2])
+        for q in range(2):
+            wp_regroup("G", q)
+
+        for t in range(NU + 3):
+            k = t - 3
+            vshare = (2, 3) if k <= 12 or k == 15 else (3,)
+            mul(t - 2)
+            for j in range(3):
+                mm2(k, j)
+            for j in range(3):
+                c_o(k, j, "V" if j in vshare else "S")
             if t >= 1:
                 q_x(t + 1)
-            q_h(t - 1)
-            if t == 0:
-                mm1(0)
-                s_g(0)
-                mm1(1)
-                s_g(1)
-                wp_prepare()
-            elif t > 1:
-                mm1(t)
-                s_g(t)
-            mm2(k, [3])
-            c_o(k, [3])
-            if k == NU - 1:
-                store(k, slice(0, 1024))
-                store(k, slice(1024, 2048))
-            else:
-                store(k, slice(0, 2048))
-            t_y(t)
-            if t == 0:
-                x_blocks(4, 6)
-            else:
-                x_blocks(2 * t + 5, 2 * t + 6)
+            q_h(t - 2)
+            for u2 in range(2):
+                mm1(t, u2)
+            for u2 in range(2):
+                s_g(t, u2)
+            if t == 2:
+                wp_quantise(0)
+                wp_quantise(1)
+            mm2(k, 3)
+            c_o(k, 3, "V" if 3 in vshare else "S")
+            store(k, 2 if k == NU - 1 else 1)
+            if not (False):
+                t_y(t - 1)
+            for q in range(2 * t + 4, 2 * t + 6):
+                t_x(q)
+            if False:
+                t_y(t - 1)
+            for q in range(2 * t + 4, 2 * t + 6):
+                c_x(q, "S")

@@ -14,20 +14,20 @@ SIGMOID = mybir.ActivationFunctionType.Sigmoid
 MULT = mybir.AluOpType.mult
 
 P = 128
-NG = 8
+NB = 4
 NU = 16
 
 
 def tile_multiheadattention_pb_t_kernel(tc, x, y_attn, w_gate, w_proj, out):
     nc = tc.nc
-    xv = x.rearrange("b (s p i) c -> (b s) p (i c)", p=P, i=4)
-    yv = y_attn.rearrange("b (s p i) h d -> (b s) p (i h d)", p=P, i=4)
-    ov = out.rearrange("b (s p i) n -> (b s) p (i n)", p=P, i=4)
+    xv = x.rearrange("b (p i) c -> b p (i c)", i=8)
+    yv = y_attn.rearrange("b (p i) h d -> b p (i h d)", i=8)
+    ov = out.rearrange("b (p i) n -> b p (i n)", i=8)
 
     with ExitStack() as ctx:
         const = ctx.enter_context(tc.tile_pool(name="const", bufs=1))
-        xpool = ctx.enter_context(tc.tile_pool(name="xpool", bufs=8))
-        ypool = ctx.enter_context(tc.tile_pool(name="ypool", bufs=8))
+        xpool = ctx.enter_context(tc.tile_pool(name="xpool", bufs=4))
+        ypool = ctx.enter_context(tc.tile_pool(name="ypool", bufs=4))
         opool = ctx.enter_context(tc.tile_pool(name="opool", bufs=8))
         work = ctx.enter_context(tc.tile_pool(name="work", bufs=4))
         ps_x = ctx.enter_context(tc.psum_pool(name="ps_x", bufs=2))
@@ -96,35 +96,32 @@ def tile_multiheadattention_pb_t_kernel(tc, x, y_attn, w_gate, w_proj, out):
 
         def load_x(g, first, last):
             if g not in x_sb:
-                x_sb[g] = xpool.tile([P, 4096], BF16, name="x_sb")
+                x_sb[g] = xpool.tile([P, 8192], BF16, name="x_sb")
             cols = slice(1024 * first, 1024 * last)
             nc.sync.dma_start(out=x_sb[g][:, cols], in_=xv[g][:, cols])
 
-        def load_y(g):
-            y_sb[g] = ypool.tile([P, 2048], BF16, name="y_sb")
-            nc.sync.dma_start(out=y_sb[g][:], in_=yv[g])
+        def load_y(g, first, last):
+            if g not in y_sb:
+                y_sb[g] = ypool.tile([P, 4096], BF16, name="y_sb")
+            cols = slice(512 * first, 512 * last)
+            nc.sync.dma_start(out=y_sb[g][:, cols], in_=yv[g][:, cols])
 
         load_wg(0)
         load_x(0, 0, 2)
         load_wg(1)
         load_x(0, 2, 4)
-        load_x(1, 0, 2)
-        load_x(1, 2, 4)
         load_wp()
-        load_y(0)
-        load_x(2, 0, 4)
-        load_y(1)
-        load_x(3, 0, 4)
-        load_y(2)
-        load_x(4, 0, 4)
-        load_y(3)
-        load_x(5, 0, 4)
-        load_y(4)
-        load_x(6, 0, 4)
-        load_y(5)
-        load_x(7, 0, 4)
-        load_y(6)
-        load_y(7)
+        load_x(0, 4, 6)
+        load_y(0, 0, 4)
+        load_x(0, 6, 8)
+        load_x(1, 0, 4)
+        load_y(0, 4, 8)
+        load_x(1, 4, 8)
+        load_y(1, 0, 8)
+        load_x(2, 0, 8)
+        load_y(2, 0, 8)
+        load_x(3, 0, 8)
+        load_y(3, 0, 8)
 
         def wg_regroup(eng, g2, u2):
             src = wg_raw[:, 2048 * g2 : 2048 * g2 + 2048].rearrange("p (j m) -> p j m", j=4)
@@ -165,8 +162,8 @@ def tile_multiheadattention_pb_t_kernel(tc, x, y_attn, w_gate, w_proj, out):
             k = q // 2
             if not live(k):
                 return
-            x32 = x_sb[k // 2][:].bitcast(F32)
-            i = q % 4
+            x32 = x_sb[k // 4][:].bitcast(F32)
+            i = q % 8
             xt[q] = bank(pool, name)
             for a in range(4):
                 nc.tensor.transpose(
@@ -229,10 +226,10 @@ def tile_multiheadattention_pb_t_kernel(tc, x, y_attn, w_gate, w_proj, out):
         def t_y(k):
             if not live(k):
                 return
-            y32 = y_sb[k // 2][:].bitcast(F32)
+            y32 = y_sb[k // 4][:].bitcast(F32)
             yt[k] = bank(ps_y, "yt")
             for b in range(2):
-                i = 2 * (k % 2) + b
+                i = 2 * (k % 4) + b
                 for u in range(2):
                     nc.tensor.transpose(
                         yt[k][:, 256 * u + 128 * b : 256 * u + 128 * b + 128],
@@ -287,18 +284,18 @@ def tile_multiheadattention_pb_t_kernel(tc, x, y_attn, w_gate, w_proj, out):
             w = 2048 // parts
             for part in range(parts):
                 lo = w * part
-                base = 2048 * (k % 2) + lo
-                nc.sync.dma_start(out=ov[k // 2][:, base : base + w], in_=ost[k][:, lo : lo + w])
+                base = 2048 * (k % 4) + lo
+                nc.sync.dma_start(out=ov[k // 4][:, base : base + w], in_=ost[k][:, lo : lo + w])
 
-        wg_regroup("V", 0, 0)
-        wg_regroup("S", 0, 1)
         for q in range(2):
             t_x(q)
         c_x(0, "S")
-        c_x(1, "V")
-        wg_quantise(0)
+        wg_regroup("V", 0, 0)
+        wg_regroup("S", 0, 1)
         wg_regroup("V", 1, 0)
         wg_regroup("S", 1, 1)
+        c_x(1, "V")
+        wg_quantise(0)
         q_x(0)
         wg_quantise(1)
         for q in range(2, 4):
@@ -306,9 +303,6 @@ def tile_multiheadattention_pb_t_kernel(tc, x, y_attn, w_gate, w_proj, out):
         for q in range(2, 4):
             c_x(q)
         q_x(1)
-        for q in range(2):
-            wp_regroup("G", q)
-
         for t in range(NU + 3):
             k = t - 3
             vshare = (2, 3) if k <= 12 or k == 15 else (3,)
@@ -324,6 +318,9 @@ def tile_multiheadattention_pb_t_kernel(tc, x, y_attn, w_gate, w_proj, out):
                 mm1(t, u2)
             for u2 in range(2):
                 s_g(t, u2)
+            if t == 0:
+                wp_regroup("V", 0)
+                wp_regroup("V", 1)
             if t == 2:
                 wp_quantise(0)
                 wp_quantise(1)

@@ -68,6 +68,8 @@ def tile_multiheadattention_pb_t_kernel(tc, x, y_attn, w_gate, w_proj, out):
         warm2 = const.tile([P, 1], F32, name="warm2")
         nc.vector.memset(warm[:], 0.0)
         nc.scalar.activation(out=warm2[:], in_=warm[:], func=SIGMOID)
+        warm_in = const.tile([P, 512], BF16, name="warm_in")
+        nc.vector.memset(warm_in[:], 0.0)
         ident = const.tile([P, P], F32, name="ident")
         make_identity(nc, ident[:])
 
@@ -154,6 +156,13 @@ def tile_multiheadattention_pb_t_kernel(tc, x, y_attn, w_gate, w_proj, out):
                 scales=wps[:, 512 * q : 512 * q + 512],
                 in_=wp_grp[:, 2048 * q : 2048 * q + 2048],
             )
+
+        def keep_warm(count):
+            for unused in range(count):
+                idle = bank(ps_o, "ot")
+                nc.tensor.matmul(
+                    out=idle[:], lhsT=warm_in[:, 0:P], rhs=warm_in[:], start=True, stop=True
+                )
 
         def live(k):
             return 0 <= k < NU
@@ -287,6 +296,7 @@ def tile_multiheadattention_pb_t_kernel(tc, x, y_attn, w_gate, w_proj, out):
                 base = 2048 * (k % 4) + lo
                 nc.sync.dma_start(out=ov[k // 4][:, base : base + w], in_=ost[k][:, lo : lo + w])
 
+        keep_warm(8)
         for q in range(2):
             t_x(q)
         c_x(0, "S")
@@ -298,11 +308,13 @@ def tile_multiheadattention_pb_t_kernel(tc, x, y_attn, w_gate, w_proj, out):
         wg_quantise(0)
         q_x(0)
         wg_quantise(1)
+        keep_warm(5)
         for q in range(2, 4):
             t_x(q)
         for q in range(2, 4):
             c_x(q)
         q_x(1)
+        keep_warm(2)
         for t in range(NU + 3):
             k = t - 3
             vshare = (2, 3) if k <= 12 or k == 15 else (3,)

@@ -73,10 +73,10 @@ def tile_multiheadattention_pb_t_kernel(tc, x, y_attn, w_gate, w_proj, out):
         ident = const.tile([P, P], F32, name="ident")
         make_identity(nc, ident[:])
 
-        wgc = const.tile([P, 1024], U32, name="wgc", align_bytes=64)
-        wgs = const.tile([P, 1024], U8, name="wgs", align_bytes=64)
-        wpc = const.tile([P, 1024], U32, name="wpc", align_bytes=64)
-        wps = const.tile([P, 1024], U8, name="wps", align_bytes=64)
+        wgc = const.tile([P, 1024], U32, name="wgc", align_bytes=256)
+        wgs = const.tile([P, 1024], U8, name="wgs", align_bytes=256)
+        wpc = const.tile([P, 1024], U32, name="wpc", align_bytes=256)
+        wps = const.tile([P, 1024], U8, name="wps", align_bytes=256)
 
         wg_raw = opool.tile([P, 4096], BF16, name="wg_raw", tag="ost", align_bytes=64)
         wp_raw = opool.tile([P, 4096], BF16, name="wp_raw", tag="ost", align_bytes=64)
@@ -108,15 +108,16 @@ def tile_multiheadattention_pb_t_kernel(tc, x, y_attn, w_gate, w_proj, out):
             cols = slice(512 * first, 512 * last)
             nc.sync.dma_start(out=y_sb[g][:, cols], in_=yv[g][:, cols])
 
-        load_wg(0)
         load_x(0, 0, 2)
+        load_wg(0)
         load_wg(1)
         load_x(0, 2, 4)
-        load_wp()
         load_x(0, 4, 6)
+        load_wp()
         load_y(0, 0, 4)
         load_x(0, 6, 8)
-        load_x(1, 0, 4)
+        load_x(1, 0, 2)
+        load_x(1, 2, 4)
         load_y(0, 4, 8)
         load_x(1, 4, 8)
         load_y(1, 0, 8)
@@ -198,8 +199,8 @@ def tile_multiheadattention_pb_t_kernel(tc, x, y_attn, w_gate, w_proj, out):
         def q_x(k):
             if not live(k):
                 return
-            xc[k] = work.tile([P, 512], U32, name="xc", align_bytes=64)
-            xs[k] = work.tile([P, 512], U8, name="xs", align_bytes=64)
+            xc[k] = work.tile([P, 512], U32, name="xc", align_bytes=256)
+            xs[k] = work.tile([P, 512], U8, name="xs", align_bytes=256)
             nc.vector.quantize_mx(out=xc[k][:].bitcast(FP8X4), scales=xs[k][:], in_=xgrp[k][:])
 
         def mm1(k, u2):
@@ -260,8 +261,8 @@ def tile_multiheadattention_pb_t_kernel(tc, x, y_attn, w_gate, w_proj, out):
         def q_h(k):
             if not live(k):
                 return
-            hc[k] = work.tile([P, 256], U32, name="hc", align_bytes=64)
-            hs[k] = work.tile([P, 256], U8, name="hs", align_bytes=64)
+            hc[k] = work.tile([P, 256], U32, name="hc", align_bytes=256)
+            hs[k] = work.tile([P, 256], U8, name="hs", align_bytes=256)
             nc.vector.quantize_mx(out=hc[k][:].bitcast(FP8X4), scales=hs[k][:], in_=hgrp[k][:])
 
         def mm2(k, j):
@@ -300,13 +301,13 @@ def tile_multiheadattention_pb_t_kernel(tc, x, y_attn, w_gate, w_proj, out):
         for q in range(2):
             t_x(q)
         c_x(0, "S")
+        c_x(1, "V")
+        q_x(0)
         wg_regroup("V", 0, 0)
         wg_regroup("S", 0, 1)
         wg_regroup("V", 1, 0)
         wg_regroup("S", 1, 1)
-        c_x(1, "V")
         wg_quantise(0)
-        q_x(0)
         wg_quantise(1)
         keep_warm(5)
         for q in range(2, 4):

@@ -324,9 +324,13 @@ def tile_multiheadattention_pb_t_kernel(tc, x, y_attn, w_gate, w_proj, out):
                 mm2(k, j)
             for j in range(3):
                 c_o(k, j, "V" if j in vshare else "S")
+            if t == 2:
+                wp_quantise(0)
+            q_h(t - 2)
+            if t == 2:
+                wp_quantise(1)
             if t >= 1:
                 q_x(t + 1)
-            q_h(t - 2)
             for u2 in range(2):
                 mm1(t, u2)
             for u2 in range(2):
@@ -334,9 +338,6 @@ def tile_multiheadattention_pb_t_kernel(tc, x, y_attn, w_gate, w_proj, out):
             if t == 0:
                 wp_regroup("V", 0)
                 wp_regroup("V", 1)
-            if t == 2:
-                wp_quantise(0)
-                wp_quantise(1)
             mm2(k, 3)
             c_o(k, 3, "V" if 3 in vshare else "S")
             store(k, 2 if k == NU - 1 else 1)

@@ -28,7 +28,7 @@ def tile_multiheadattention_pb_t_kernel(tc, x, y_attn, w_gate, w_proj, out):
         const = ctx.enter_context(tc.tile_pool(name="const", bufs=1))
         xpool = ctx.enter_context(tc.tile_pool(name="xpool", bufs=4))
         ypool = ctx.enter_context(tc.tile_pool(name="ypool", bufs=4))
-        opool = ctx.enter_context(tc.tile_pool(name="opool", bufs=8))
+        opool = ctx.enter_context(tc.tile_pool(name="opool", bufs=4))
         work = ctx.enter_context(tc.tile_pool(name="work", bufs=4))
         ps_x = ctx.enter_context(tc.psum_pool(name="ps_x", bufs=2))
         ps_y = ctx.enter_context(tc.psum_pool(name="ps_y", bufs=1))
@@ -78,10 +78,12 @@ def tile_multiheadattention_pb_t_kernel(tc, x, y_attn, w_gate, w_proj, out):
         wpc = const.tile([P, 1024], U32, name="wpc", align_bytes=256)
         wps = const.tile([P, 1024], U8, name="wps", align_bytes=256)
 
-        wg_raw = opool.tile([P, 4096], BF16, name="wg_raw", tag="ost", align_bytes=64)
-        wp_raw = opool.tile([P, 4096], BF16, name="wp_raw", tag="ost", align_bytes=64)
-        wg_grp = opool.tile([P, 4096], BF16, name="wg_grp", tag="ost", align_bytes=64)
-        wp_grp = opool.tile([P, 4096], BF16, name="wp_grp", tag="ost", align_bytes=64)
+        w_raw = opool.tile([P, 8192], BF16, name="w_raw", tag="ost", align_bytes=256)
+        w_grp = opool.tile([P, 8192], BF16, name="w_grp", tag="ost", align_bytes=256)
+        wg_raw = w_raw[:, 0:4096]
+        wp_raw = w_raw[:, 4096:8192]
+        wg_grp = w_grp[:, 0:4096]
+        wp_grp = w_grp[:, 4096:8192]
         wgv = w_gate.rearrange("(a q e) m -> q a (e m)", a=4, q=P, e=2)
 
         def load_wg(g2):
@@ -92,19 +94,19 @@ def tile_multiheadattention_pb_t_kernel(tc, x, y_attn, w_gate, w_proj, out):
 
         def load_wp():
             nc.sync.dma_start(
-                out=wp_raw[:].rearrange("p (u r) -> p u r", u=2),
+                out=wp_raw.rearrange("p (u r) -> p u r", u=2),
                 in_=w_proj.rearrange("(u q e) n -> q u (e n)", u=2, q=P, e=2),
             )
 
         def load_x(g, first, last):
             if g not in x_sb:
-                x_sb[g] = xpool.tile([P, 8192], BF16, name="x_sb")
+                x_sb[g] = xpool.tile([P, 8192], BF16, name="x_sb", align_bytes=256)
             cols = slice(1024 * first, 1024 * last)
             nc.sync.dma_start(out=x_sb[g][:, cols], in_=xv[g][:, cols])
 
         def load_y(g, first, last):
             if g not in y_sb:
-                y_sb[g] = ypool.tile([P, 4096], BF16, name="y_sb")
+                y_sb[g] = ypool.tile([P, 4096], BF16, name="y_sb", align_bytes=256)
             cols = slice(512 * first, 512 * last)
             nc.sync.dma_start(out=y_sb[g][:, cols], in_=yv[g][:, cols])
 
@@ -146,7 +148,7 @@ def tile_multiheadattention_pb_t_kernel(tc, x, y_attn, w_gate, w_proj, out):
             copy_on(
                 eng,
                 wp_grp[:, 2048 * q : 2048 * q + 2048].rearrange("p (c i t) -> p c t i", i=4, t=4),
-                wp_raw[:]
+                wp_raw
                 .rearrange("p (t n) -> p t n", t=4)[:, :, 512 * q : 512 * q + 512]
                 .rearrange("p t (c i) -> p c t i", i=4),
             )
@@ -268,9 +270,10 @@ def tile_multiheadattention_pb_t_kernel(tc, x, y_attn, w_gate, w_proj, out):
         def mm2(k, j):
             if not live(k):
                 return
+            spare = k + 3 >= 14 and j == 3
             tcols = slice(128 * (j // 2), 128 * (j // 2) + 128)
             ncols = slice(512 * (j % 2), 512 * (j % 2) + 512)
-            ot[(k, j)] = bank(ps_o, "ot")
+            ot[(k, j)] = bank(ps_x, "xt") if spare else bank(ps_o, "ot")
             nc.tensor.matmul_mx(
                 out=ot[(k, j)][:],
                 lhsT=hc[k][:, tcols].bitcast(FP8X4),
@@ -284,18 +287,21 @@ def tile_multiheadattention_pb_t_kernel(tc, x, y_attn, w_gate, w_proj, out):
         def c_o(k, j, eng):
             if not live(k):
                 return
-            if k not in ost:
-                ost[k] = opool.tile([P, 2048], F32, name="ost", tag="ost", align_bytes=64)
-            copy_on(eng, ost[k][:, 512 * j : 512 * j + 512], ot[(k, j)][:])
+            pair = k // 2
+            if pair not in ost:
+                ost[pair] = opool.tile([P, 4096], F32, name="ost", tag="ost", align_bytes=256)
+            col = 2048 * (k % 2) + 512 * j
+            copy_on(eng, ost[pair][:, col : col + 512], ot[(k, j)][:])
 
-        def store(k, parts=1):
+        def store(k, first, last):
             if not live(k):
                 return
-            w = 2048 // parts
-            for part in range(parts):
-                lo = w * part
-                base = 2048 * (k % 4) + lo
-                nc.sync.dma_start(out=ov[k // 4][:, base : base + w], in_=ost[k][:, lo : lo + w])
+            pair = k // 2
+            base = 4096 * (pair % 2)
+            nc.sync.dma_start(
+                out=ov[pair // 2][:, base + 512 * first : base + 512 * last],
+                in_=ost[pair][:, 512 * first : 512 * last],
+            )
 
         keep_warm(8)
         for q in range(2):
@@ -331,6 +337,15 @@ def tile_multiheadattention_pb_t_kernel(tc, x, y_attn, w_gate, w_proj, out):
                 wp_quantise(1)
             if t >= 1:
                 q_x(t + 1)
+            if t >= 14:
+                mm2(k, 3)
+                c_o(k, 3, "V" if 3 in vshare else "S")
+                if k == NU - 1:
+                    store(k, 4, 8)
+                elif k >= 10:
+                    store(k, 4 * (k % 2), 4 * (k % 2) + 4)
+                elif k % 2 == 1:
+                    store(k, 0, 8)
             for u2 in range(2):
                 mm1(t, u2)
             for u2 in range(2):
@@ -338,9 +353,15 @@ def tile_multiheadattention_pb_t_kernel(tc, x, y_attn, w_gate, w_proj, out):
             if t == 0:
                 wp_regroup("V", 0)
                 wp_regroup("V", 1)
-            mm2(k, 3)
-            c_o(k, 3, "V" if 3 in vshare else "S")
-            store(k, 2 if k == NU - 1 else 1)
+            if not (t >= 14):
+                mm2(k, 3)
+                c_o(k, 3, "V" if 3 in vshare else "S")
+                if k == NU - 1:
+                    store(k, 4, 8)
+                elif k >= 10:
+                    store(k, 4 * (k % 2), 4 * (k % 2) + 4)
+                elif k % 2 == 1:
+                    store(k, 0, 8)
             if not (False):
                 t_y(t - 1)
             for q in range(2 * t + 4, 2 * t + 6):

@@ -114,12 +114,11 @@ def tile_multiheadattention_pb_t_kernel(tc, x, y_attn, w_gate, w_proj, out):
         load_wg(0)
         load_wg(1)
         load_x(0, 2, 4)
-        load_x(0, 4, 6)
         load_wp()
+        load_x(0, 4, 6)
         load_y(0, 0, 4)
         load_x(0, 6, 8)
-        load_x(1, 0, 2)
-        load_x(1, 2, 4)
+        load_x(1, 0, 4)
         load_y(0, 4, 8)
         load_x(1, 4, 8)
         load_y(1, 0, 8)

@@ -136,11 +136,12 @@ def tile_multiheadattention_pb_t_kernel(tc, x, y_attn, w_gate, w_proj, out):
                 src[:, :, 256 * u2 : 256 * u2 + 256].rearrange("p j (p2 e2) -> p e2 p2 j", e2=2),
             )
 
-        def wg_quantise(g2):
+        def wg_quantise(g2, u2):
+            base = 512 * g2 + 256 * u2
             nc.vector.quantize_mx(
-                out=wgc[:, 512 * g2 : 512 * g2 + 512].bitcast(FP8X4),
-                scales=wgs[:, 512 * g2 : 512 * g2 + 512],
-                in_=wg_grp[:, 2048 * g2 : 2048 * g2 + 2048],
+                out=wgc[:, base : base + 256].bitcast(FP8X4),
+                scales=wgs[:, base : base + 256],
+                in_=wg_grp[:, 4 * base : 4 * base + 1024],
             )
 
         def wp_regroup(eng, q):
@@ -307,13 +308,15 @@ def tile_multiheadattention_pb_t_kernel(tc, x, y_attn, w_gate, w_proj, out):
             t_x(q)
         c_x(0, "S")
         c_x(1, "V")
-        q_x(0)
         wg_regroup("V", 0, 0)
         wg_regroup("S", 0, 1)
         wg_regroup("V", 1, 0)
+        wg_quantise(0, 0)
+        q_x(0)
+        wg_quantise(1, 0)
         wg_regroup("S", 1, 1)
-        wg_quantise(0)
-        wg_quantise(1)
+        wg_quantise(0, 1)
+        wg_quantise(1, 1)
         keep_warm(5)
         for q in range(2, 4):
             t_x(q)
@@ -341,7 +344,7 @@ def tile_multiheadattention_pb_t_kernel(tc, x, y_attn, w_gate, w_proj, out):
                 c_o(k, 3, "V" if 3 in vshare else "S")
                 if k == NU - 1:
                     store(k, 4, 8)
-                elif k >= 10:
+                elif k >= 8:
                     store(k, 4 * (k % 2), 4 * (k % 2) + 4)
                 elif k % 2 == 1:
                     store(k, 0, 8)
@@ -357,7 +360,7 @@ def tile_multiheadattention_pb_t_kernel(tc, x, y_attn, w_gate, w_proj, out):
                 c_o(k, 3, "V" if 3 in vshare else "S")
                 if k == NU - 1:
                     store(k, 4, 8)
-                elif k >= 10:
+                elif k >= 8:
                     store(k, 4 * (k % 2), 4 * (k % 2) + 4)
                 elif k % 2 == 1:
                     store(k, 0, 8)

from contextlib import ExitStack

import concourse.mybir as mybir
from concourse.masks import make_identity

FLOPS = 2 * 4096 * 1024 * 512 * 2

BF16 = mybir.dt.bfloat16
F32 = mybir.dt.float32
U32 = mybir.dt.uint32
U8 = mybir.dt.uint8
FP8X4 = mybir.dt.float8_e4m3fn_x4
SIGMOID = mybir.ActivationFunctionType.Sigmoid
MULT = mybir.AluOpType.mult

P = 128
NB = 4
NU = 16


def tile_multiheadattention_pb_t_kernel(tc, x, y_attn, w_gate, w_proj, out):
    nc = tc.nc
    xv = x.rearrange("b (p i) c -> b p (i c)", i=8)
    yv = y_attn.rearrange("b (p i) h d -> b p (i h d)", i=8)
    ov = out.rearrange("b (p i) n -> b p (i n)", i=8)

    with ExitStack() as ctx:
        const = ctx.enter_context(tc.tile_pool(name="const", bufs=1))
        xpool = ctx.enter_context(tc.tile_pool(name="xpool", bufs=4))
        ypool = ctx.enter_context(tc.tile_pool(name="ypool", bufs=4))
        opool = ctx.enter_context(tc.tile_pool(name="opool", bufs=4))
        work = ctx.enter_context(tc.tile_pool(name="work", bufs=4))
        ps_x = ctx.enter_context(tc.psum_pool(name="ps_x", bufs=2))
        ps_y = ctx.enter_context(tc.psum_pool(name="ps_y", bufs=1))
        ps_g = ctx.enter_context(tc.psum_pool(name="ps_g", bufs=2))
        ps_o = ctx.enter_context(tc.psum_pool(name="ps_o", bufs=3))
        ctx.enter_context(tc.manual_schedule())

        x_sb = {}
        y_sb = {}
        xt = {}
        yt = {}
        gt = {}
        ot = {}
        xgrp = {}
        xc = {}
        xs = {}
        sig = {}
        hgrp = {}
        hc = {}
        hs = {}
        ost = {}

        def bank(pool, name):
            return pool.tile([P, 512], F32, name="bank", tag=name)

        def copy_on(eng, dst, src):
            if eng == "G":
                nc.gpsimd.tensor_scalar(
                    out=dst, in0=src, scalar1=1.0, scalar2=0.0, op0=MULT, op1=mybir.AluOpType.add
                )
            elif eng == "V":
                nc.vector.tensor_copy(out=dst, in_=src)
            else:
                nc.scalar.copy(out=dst, in_=src)

        warm = const.tile([P, 1], F32, name="warm")
        warm2 = const.tile([P, 1], F32, name="warm2")
        nc.vector.memset(warm[:], 0.0)
        nc.scalar.activation(out=warm2[:], in_=warm[:], func=SIGMOID)
        warm_in = const.tile([P, 512], BF16, name="warm_in")
        nc.vector.memset(warm_in[:], 0.0)
        ident = const.tile([P, P], F32, name="ident")
        make_identity(nc, ident[:])

        wgc = const.tile([P, 1024], U32, name="wgc", align_bytes=256)
        wgs = const.tile([P, 1024], U8, name="wgs", align_bytes=256)
        wpc = const.tile([P, 1024], U32, name="wpc", align_bytes=256)
        wps = const.tile([P, 1024], U8, name="wps", align_bytes=256)

        w_raw = opool.tile([P, 8192], BF16, name="w_raw", tag="ost", align_bytes=256)
        w_grp = opool.tile([P, 8192], BF16, name="w_grp", tag="ost", align_bytes=256)
        wg_raw = w_raw[:, 0:4096]
        wp_raw = w_raw[:, 4096:8192]
        wg_grp = w_grp[:, 0:4096]
        wp_grp = w_grp[:, 4096:8192]
        wgv = w_gate.rearrange("(a q e) m -> q a (e m)", a=4, q=P, e=2)

        def load_wg(g2):
            nc.sync.dma_start(
                out=wg_raw[:, 2048 * g2 : 2048 * g2 + 2048].rearrange("p (a r) -> p a r", a=2),
                in_=wgv[:, 2 * g2 : 2 * g2 + 2, :],
            )

        def load_wp():
            nc.sync.dma_start(
                out=wp_raw.rearrange("p (u r) -> p u r", u=2),
                in_=w_proj.rearrange("(u q e) n -> q u (e n)", u=2, q=P, e=2),
            )

        def load_x(g, first, last):
            if g not in x_sb:
                x_sb[g] = xpool.tile([P, 8192], BF16, name="x_sb", align_bytes=256)
            cols = slice(1024 * first, 1024 * last)
            nc.sync.dma_start(out=x_sb[g][:, cols], in_=xv[g][:, cols])

        def load_y(g, first, last):
            if g not in y_sb:
                y_sb[g] = ypool.tile([P, 4096], BF16, name="y_sb", align_bytes=256)
            cols = slice(512 * first, 512 * last)
            nc.sync.dma_start(out=y_sb[g][:, cols], in_=yv[g][:, cols])

        load_x(0, 0, 2)
        load_wg(0)
        load_wg(1)
        load_x(0, 2, 4)
        load_wp()
        load_x(0, 4, 6)
        load_y(0, 0, 4)
        load_x(0, 6, 8)
        load_x(1, 0, 4)
        load_y(0, 4, 8)
        load_x(1, 4, 8)
        load_y(1, 0, 8)
        load_x(2, 0, 8)
        load_y(2, 0, 8)
        load_x(3, 0, 8)
        load_y(3, 0, 8)

        def wg_regroup(eng, g2, u2):
            src = wg_raw[:, 2048 * g2 : 2048 * g2 + 2048].rearrange("p (j m) -> p j m", j=4)
            base = 2048 * g2 + 1024 * u2
            copy_on(
                eng,
                wg_grp[:, base : base + 1024].rearrange("p (e2 p2 j) -> p e2 p2 j", e2=2, j=4),
                src[:, :, 256 * u2 : 256 * u2 + 256].rearrange("p j (p2 e2) -> p e2 p2 j", e2=2),
            )

        def wg_quantise(g2, u2):
            base = 512 * g2 + 256 * u2
            nc.vector.quantize_mx(
                out=wgc[:, base : base + 256].bitcast(FP8X4),
                scales=wgs[:, base : base + 256],
                in_=wg_grp[:, 4 * base : 4 * base + 1024],
            )

        def wp_regroup(eng, q):
            copy_on(
                eng,
                wp_grp[:, 2048 * q : 2048 * q + 2048].rearrange("p (c i t) -> p c t i", i=4, t=4),
                wp_raw
                .rearrange("p (t n) -> p t n", t=4)[:, :, 512 * q : 512 * q + 512]
                .rearrange("p t (c i) -> p c t i", i=4),
            )

        def wp_quantise(q):
            nc.vector.quantize_mx(
                out=wpc[:, 512 * q : 512 * q + 512].bitcast(FP8X4),
                scales=wps[:, 512 * q : 512 * q + 512],
                in_=wp_grp[:, 2048 * q : 2048 * q + 2048],
            )

        def keep_warm(count):
            for unused in range(count):
                idle = bank(ps_o, "ot")
                nc.tensor.matmul(
                    out=idle[:], lhsT=warm_in[:, 0:P], rhs=warm_in[:], start=True, stop=True
                )

        def live(k):
            return 0 <= k < NU

        def t_x(q, pool=ps_x, name="xt"):
            k = q // 2
            if not live(k):
                return
            x32 = x_sb[k // 4][:].bitcast(F32)
            i = q % 8
            xt[q] = bank(pool, name)
            for a in range(4):
                nc.tensor.transpose(
                    xt[q][:, 128 * a : 128 * a + 128],
                    x32[:, 512 * i + 128 * a : 512 * i + 128 * a + 128],
                    ident[:],
                )

        def c_x(q, eng="S"):
            k = q // 2
            if not live(k):
                return
            b = q % 2
            if k not in xgrp:
                xgrp[k] = work.tile([P, 2048], BF16, name="xgrp", align_bytes=64)
            xg32 = xgrp[k][:].bitcast(F32).rearrange("p (g t u) -> p g t u", g=2, u=2)
            copy_on(
                eng,
                xg32[:, :, 128 * b : 128 * b + 128, :],
                xt[q][:].rearrange("p (g u t) -> p g t u", g=2, u=2),
            )

        def q_x(k):
            if not live(k):
                return
            xc[k] = work.tile([P, 512], U32, name="xc", align_bytes=256)
            xs[k] = work.tile([P, 512], U8, name="xs", align_bytes=256)
            nc.vector.quantize_mx(out=xc[k][:].bitcast(FP8X4), scales=xs[k][:], in_=xgrp[k][:])

        def mm1(k, u2):
            if not live(k):
                return
            gt[(k, u2)] = bank(ps_g, "gt")
            for e2 in range(2):
                m = 2 * u2 + e2
                for g2 in range(2):
                    wcols = slice(512 * g2 + 128 * m, 512 * g2 + 128 * m + 128)
                    xcols = slice(256 * g2, 256 * g2 + 256)
                    nc.tensor.matmul_mx(
                        out=gt[(k, u2)][:, 256 * e2 : 256 * e2 + 256],
                        lhsT=wgc[:, wcols].bitcast(FP8X4),
                        lhsT_scale=wgs[:, wcols],
                        rhs=xc[k][:, xcols].bitcast(FP8X4),
                        rhs_scale=xs[k][:, xcols],
                        start=(g2 == 0),
                        stop=(g2 == 1),
                    )

        def s_g(k, u2):
            if not live(k):
                return
            if u2 == 0:
                sig[k] = work.tile([P, 1024], F32, name="sig")
            nc.scalar.activation(
                out=sig[k][:, 512 * u2 : 512 * u2 + 512].rearrange("p (t e) -> p t e", e=2),
                in_=gt[(k, u2)][:].rearrange("p (e t) -> p t e", e=2),
                func=SIGMOID,
            )

        def t_y(k):
            if not live(k):
                return
            y32 = y_sb[k // 4][:].bitcast(F32)
            yt[k] = bank(ps_y, "yt")
            for b in range(2):
                i = 2 * (k % 4) + b
                for u in range(2):
                    nc.tensor.transpose(
                        yt[k][:, 256 * u + 128 * b : 256 * u + 128 * b + 128],
                        y32[:, 256 * i + 128 * u : 256 * i + 128 * u + 128],
                        ident[:],
                    )

        def mul(k):
            if not live(k):
                return
            hgrp[k] = work.tile([P, 1024], BF16, name="hgrp", align_bytes=64)
            nc.vector.tensor_tensor(
                out=hgrp[k][:].rearrange("p (t u e) -> p t u e", u=2, e=2),
                in0=sig[k][:].rearrange("p (u t e) -> p t u e", u=2, e=2),
                in1=yt[k][:].bitcast(BF16).rearrange("p (u t e) -> p t u e", u=2, e=2),
                op=MULT,
            )

        def q_h(k):
            if not live(k):
                return
            hc[k] = work.tile([P, 256], U32, name="hc", align_bytes=256)
            hs[k] = work.tile([P, 256], U8, name="hs", align_bytes=256)
            nc.vector.quantize_mx(out=hc[k][:].bitcast(FP8X4), scales=hs[k][:], in_=hgrp[k][:])

        def mm2(k, j):
            if not live(k):
                return
            spare = k + 3 >= 14 and j == 3
            tcols = slice(128 * (j // 2), 128 * (j // 2) + 128)
            ncols = slice(512 * (j % 2), 512 * (j % 2) + 512)
            ot[(k, j)] = bank(ps_x, "xt") if spare else bank(ps_o, "ot")
            nc.tensor.matmul_mx(
                out=ot[(k, j)][:],
                lhsT=hc[k][:, tcols].bitcast(FP8X4),
                lhsT_scale=hs[k][:, tcols],
                rhs=wpc[:, ncols].bitcast(FP8X4),
                rhs_scale=wps[:, ncols],
                start=True,
                stop=True,
            )

        def c_o(k, j, eng):
            if not live(k):
                return
            pair = k // 2
            if pair not in ost:
                ost[pair] = opool.tile([P, 4096], F32, name="ost", tag="ost", align_bytes=256)
            col = 2048 * (k % 2) + 512 * j
            copy_on(eng, ost[pair][:, col : col + 512], ot[(k, j)][:])

        def store(k, first, last):
            if not live(k):
                return
            pair = k // 2
            base = 4096 * (pair % 2)
            nc.sync.dma_start(
                out=ov[pair // 2][:, base + 512 * first : base + 512 * last],
                in_=ost[pair][:, 512 * first : 512 * last],
            )

        keep_warm(8)
        for q in range(2):
            t_x(q)
        c_x(0, "S")
        c_x(1, "V")
        wg_regroup("V", 0, 0)
        wg_regroup("S", 0, 1)
        wg_regroup("V", 1, 0)
        wg_quantise(0, 0)
        q_x(0)
        wg_quantise(1, 0)
        wg_regroup("S", 1, 1)
        wg_quantise(0, 1)
        wg_quantise(1, 1)
        keep_warm(5)
        for q in range(2, 4):
            t_x(q)
        for q in range(2, 4):
            c_x(q)
        q_x(1)
        keep_warm(2)
        for t in range(NU + 3):
            k = t - 3
            vshare = (2, 3) if k <= 12 or k == 15 else (3,)
            mul(t - 2)
            for j in range(3):
                mm2(k, j)
            for j in range(3):
                c_o(k, j, "V" if j in vshare else "S")
            if t == 2:
                wp_quantise(0)
            q_h(t - 2)
            if t == 2:
                wp_quantise(1)
            if t >= 1:
                q_x(t + 1)
            if t >= 14:
                mm2(k, 3)
                c_o(k, 3, "V" if 3 in vshare else "S")
                if k == NU - 1:
                    store(k, 4, 8)
                elif k >= 8:
                    store(k, 4 * (k % 2), 4 * (k % 2) + 4)
                elif k % 2 == 1:
                    store(k, 0, 8)
            for u2 in range(2):
                mm1(t, u2)
            for u2 in range(2):
                s_g(t, u2)
            if t == 0:
                wp_regroup("V", 0)
                wp_regroup("V", 1)
            if not (t >= 14):
                mm2(k, 3)
                c_o(k, 3, "V" if 3 in vshare else "S")
                if k == NU - 1:
                    store(k, 4, 8)
                elif k >= 8:
                    store(k, 4 * (k % 2), 4 * (k % 2) + 4)
                elif k % 2 == 1:
                    store(k, 0, 8)
            if not (False):
                t_y(t - 1)
            for q in range(2 * t + 4, 2 * t + 6):
                t_x(q)
            if False:
                t_y(t - 1)
            for q in range(2 * t + 4, 2 * t + 6):
                c_x(q, "S")
